import numpy as np
import ml_dtypes


def mxq(x, axis, fmt="e4m3"):
    dtype, down = {"e4m3": (ml_dtypes.float8_e4m3fn, 7), "e5m2": (ml_dtypes.float8_e5m2, 14)}[fmt]
    v = np.moveaxis(np.asarray(x, np.float32).astype(ml_dtypes.bfloat16).astype(np.float64), axis, -1)
    blocks = v.reshape(v.shape[:-1] + (-1, 32))
    amax = np.abs(blocks).max(-1, keepdims=True)
    byte = np.maximum(np.where(amax > 0, np.frexp(amax)[1] - 1 + 127, 0) - down, 1)
    scale = np.exp2(byte - 127.0)
    codes = (blocks / scale).astype(np.float32).astype(dtype).astype(np.float64)
    return np.moveaxis((codes * scale).reshape(v.shape), -1, axis)


WIDE = False


def mx_kscale(k):
    if not WIDE:
        return np.ones(k)
    levels = np.array([10, -10, 5, -5, 0])
    a = np.random.permutation(np.resize(levels, k // 512 * 4)).reshape(k // 512, 4)
    idx = np.arange(k)
    return np.exp2(a[idx // 512, idx % 128 // 32])


BF16 = ml_dtypes.bfloat16


def bf(x):
    return np.asarray(x, np.float32).astype(BF16)


def f64(x):
    return np.asarray(x).astype(np.float64)


N, V, E1, E2, C, T, EMB = 512, 4096, 16384, 512, 128, 512, 1024
BN_EPS = 1e-5


def softplus(v):
    return np.log(1.0 + np.exp(v))


def bn(x, gamma, beta):
    m = x.mean(0)
    v = x.var(0)
    return (x - m) / np.sqrt(v + BN_EPS) * gamma + beta


def setup_inputs():
    s = mx_kscale(E1)
    return {"en1": bf(softplus(np.random.standard_normal((N, E1))) * s),
            "eps": bf(np.random.standard_normal((N, C))),
            "W2": bf(np.random.standard_normal((E2, E1)) / np.sqrt(E1) / s[None, :]),
            "b2": bf(np.random.standard_normal(E2) * 0.3),
            "Wm": bf(np.random.standard_normal((C, E2)) / np.sqrt(E2)),
            "Wv": bf(np.random.standard_normal((C, E2)) / np.sqrt(E2)),
            "gm": bf(0.5 * (1.0 + 0.1 * np.random.standard_normal(C))),
            "betam": bf(np.random.standard_normal(C) * 0.1),
            "gv": bf(0.5 * (1.0 + 0.1 * np.random.standard_normal(C))),
            "betav": bf(-1.5 + 0.1 * np.random.standard_normal(C))}


def reference(en1, eps, W2, b2, Wm, Wv, gm, betam, gv, betav):
    en2 = softplus((mxq(f64(en1), 1, "e4m3") @ mxq(f64(W2), 1, "e4m3").T) + f64(b2))
    en2q = mxq(en2, 1, "e4m3")
    posterior_mean = bn(en2q @ mxq(f64(Wm), 1, "e4m3").T, f64(gm), f64(betam))
    posterior_logvar = bn(en2q @ mxq(f64(Wv), 1, "e4m3").T, f64(gv), f64(betav))
    posterior_var = np.exp(posterior_logvar)
    return posterior_mean + np.sqrt(posterior_var) * f64(eps)

@@ -1,0 +1,244 @@
+from contextlib import ExitStack
+
+import concourse.mybir as mybir
+from concourse.masks import make_identity
+
+F32 = mybir.dt.float32
+BF16 = mybir.dt.bfloat16
+U32 = mybir.dt.uint32
+U8 = mybir.dt.uint8
+FP8X4 = mybir.dt.float8_e4m3fn_x4
+ALU = mybir.AluOpType
+ACT = mybir.ActivationFunctionType
+
+P = 128
+N = 512
+E1 = 16384
+E2 = 512
+C = 128
+K_PASS = 512
+PASSES = E1 // K_PASS
+ROWS = 4
+WORDS = K_PASS // 2
+CHUNK_PASSES = 2
+CHUNK = CHUNK_PASSES * K_PASS
+BN_EPS = 1e-5
+EXP_CAP = 30.0
+
+FLOPS = 2 * N * E1 * E2 + 2 * 2 * N * E2 * C
+
+
+def transpose_pass(nc, psum, words, first_word, ident):
+    banks = []
+    for b in range(2):
+        bank = psum.tile([P, 2, 2, P], F32, tag="bank", name="bank")
+        for s in range(2):
+            for u in range(2):
+                start = first_word + P * u
+                nc.tensor.transpose(bank[:, s, u, :], words[:, 2 * b + s, start : start + P], ident[:])
+        banks.append(bank)
+    return banks
+
+
+def bank_to_grouped(copy, grouped, b, bank):
+    half = grouped[:].bitcast(F32)[:, 4 * P * b : 4 * P * (b + 1)]
+    copy(
+        out=half.rearrange("q (s r u) -> q s r u", s=2, u=2),
+        in_=bank[:].rearrange("q s u r -> q s r u"),
+    )
+
+
+def tile_model_pa_k_kernel(tc, en1, eps, W2, b2, Wm, Wv, gm, betam, gv, betav, out):
+    nc = tc.nc
+    with ExitStack() as ctx:
+        ctx.enter_context(tc.manual_schedule())
+        const = ctx.enter_context(tc.tile_pool(name="const", bufs=1))
+        raw = ctx.enter_context(tc.tile_pool(name="raw", bufs=4))
+        stage = ctx.enter_context(tc.tile_pool(name="stage", bufs=3))
+        tail = ctx.enter_context(tc.tile_pool(name="tail", bufs=1))
+        psum_acc = ctx.enter_context(tc.psum_pool(name="psum_acc", bufs=1))
+        psum = ctx.enter_context(tc.psum_pool(name="psum", bufs=4))
+
+        en1_rows = en1.rearrange("(p i) k -> p i k", i=ROWS)
+        w2_rows = W2.rearrange("(p i) k -> p i k", i=ROWS)
+
+        wmv_raw = const.tile([P, 2, E2], BF16)
+        nc.scalar.dma_start(out=wmv_raw[:, 0, :], in_=Wm)
+        nc.scalar.dma_start(out=wmv_raw[:, 1, :], in_=Wv)
+        eps_raw = const.tile([P, ROWS, C], BF16)
+        nc.scalar.dma_start(out=eps_raw[:], in_=eps.rearrange("(p i) c -> p i c", i=ROWS))
+
+        ident = const.tile([P, P], F32)
+        make_identity(nc, ident[:])
+
+        b2_raw = const.tile([P, ROWS], BF16)
+        gm_raw = const.tile([P, 1], BF16)
+        gv_raw = const.tile([P, 1], BF16)
+        betam_raw = const.tile([P, 1], BF16)
+        betav_raw = const.tile([P, 1], BF16)
+        with nc.allow_non_contiguous_dma(reason="one or four elements a partition, once"):
+            nc.gpsimd.dma_start(out=b2_raw[:], in_=b2.rearrange("(p i) -> p i", i=ROWS))
+            nc.gpsimd.dma_start(out=gm_raw[:], in_=gm.rearrange("(p o) -> p o", o=1))
+            nc.gpsimd.dma_start(out=gv_raw[:], in_=gv.rearrange("(p o) -> p o", o=1))
+            nc.gpsimd.dma_start(out=betam_raw[:], in_=betam.rearrange("(p o) -> p o", o=1))
+            nc.gpsimd.dma_start(out=betav_raw[:], in_=betav.rearrange("(p o) -> p o", o=1))
+        b2_f32 = const.tile([P, ROWS], F32)
+        gamma = const.tile([P, 2], F32)
+        beta = const.tile([P, 2], F32)
+        for dst, src, factor in (
+            (b2_f32[:], b2_raw, 1.0),
+            (gamma[:, 0:1], gm_raw, 1.0),
+            (gamma[:, 1:2], gv_raw, 0.5),
+            (beta[:, 0:1], betam_raw, 1.0),
+            (beta[:, 1:2], betav_raw, 0.5),
+        ):
+            nc.gpsimd.tensor_scalar(out=dst, in0=src[:], scalar1=factor, scalar2=0.0, op0=ALU.mult, op1=ALU.add)
+
+        warm_in = const.tile([P, 1], F32)
+        warm_out = const.tile([P, 1], F32)
+        nc.vector.memset(warm_in[:], 0.0)
+        nc.scalar.activation(out=warm_out[:], in_=warm_in[:], func=ACT.Exp)
+        neg_half = const.tile([P, 2], F32)
+        nc.vector.memset(neg_half[:], -0.5)
+
+        eps_f32 = const.tile([P, ROWS, C], F32)
+        nc.vector.tensor_copy(out=eps_f32[:], in_=eps_raw[:])
+
+        wmv_words = wmv_raw[:].bitcast(F32).rearrange("c w (p u) -> c w u p", u=2)
+        wmv_bank = psum.tile([P, 2, 2, P], F32, tag="bank", name="wmv_bank")
+        for w in range(2):
+            for u in range(2):
+                nc.tensor.transpose(wmv_bank[:, w, u, :], wmv_words[:, w, u, :], ident[:])
+        wmv_grouped = const.tile([P, 2 * C * 4], BF16, align_bytes=64)
+        nc.vector.tensor_copy(
+            out=wmv_grouped[:].bitcast(F32).rearrange("q (w c u) -> q w c u", w=2, u=2),
+            in_=wmv_bank[:].rearrange("q w u c -> q w c u"),
+        )
+
+        eps_bank = psum.tile([P, ROWS, P], F32, tag="bank", name="eps_bank")
+        for i in range(ROWS):
+            nc.tensor.transpose(eps_bank[:, i, :], eps_f32[:, i, :], ident[:])
+        eps_t = const.tile([P, ROWS, P], F32)
+        nc.scalar.copy(out=eps_t[:], in_=eps_bank[:])
+
+        wmv_codes = const.tile([P, 2 * C], U32, align_bytes=64)
+        wmv_scales = const.tile([P, 2 * C], U8, align_bytes=64)
+        nc.vector.quantize_mx(out=wmv_codes[:].bitcast(FP8X4), scales=wmv_scales[:], in_=wmv_grouped[:])
+
+
+        acc = [psum_acc.tile([P, N], F32, name="acc%d" % j) for j in range(ROWS)]
+
+        def multiply(g, x_codes, x_scales, w_codes, w_scales):
+            for j in range(ROWS):
+                cols = slice(P * j, P * (j + 1))
+                nc.tensor.matmul_mx(
+                    out=acc[j][:],
+                    lhsT=w_codes[:, cols].bitcast(FP8X4),
+                    lhsT_scale=w_scales[:, cols],
+                    rhs=x_codes[:].bitcast(FP8X4),
+                    rhs_scale=x_scales[:],
+                    start=(g == 0),
+                    stop=(g == PASSES - 1),
+                )
+
+        for g in range(PASSES):
+            if g % CHUNK_PASSES == 0:
+                k_cols = slice(K_PASS * g, K_PASS * g + CHUNK)
+                x_raw = raw.tile([P, ROWS, CHUNK], BF16)
+                nc.sync.dma_start(out=x_raw[:], in_=en1_rows[:, :, k_cols])
+                w_raw = raw.tile([P, ROWS, CHUNK], BF16)
+                nc.sync.dma_start(out=w_raw[:], in_=w2_rows[:, :, k_cols])
+            first_word = WORDS * (g % CHUNK_PASSES)
+
+            x_banks = transpose_pass(nc, psum, x_raw[:].bitcast(F32), first_word, ident)
+            w_banks = transpose_pass(nc, psum, w_raw[:].bitcast(F32), first_word, ident)
+            if g > 0:
+                multiply(g - 1, x_codes, x_scales, w_codes, w_scales)
+
+            x_grouped = stage.tile([P, 4 * N], BF16, align_bytes=64)
+            w_grouped = stage.tile([P, 4 * E2], BF16, align_bytes=64)
+            bank_to_grouped(nc.scalar.copy, x_grouped, 0, x_banks[0])
+            bank_to_grouped(nc.scalar.copy, x_grouped, 1, x_banks[1])
+            bank_to_grouped(nc.scalar.copy, w_grouped, 0, w_banks[0])
+            bank_to_grouped(nc.vector.tensor_copy, w_grouped, 1, w_banks[1])
+
+            x_codes = stage.tile([P, N], U32, align_bytes=64)
+            x_scales = stage.tile([P, N], U8, align_bytes=64)
+            w_codes = stage.tile([P, E2], U32, align_bytes=64)
+            w_scales = stage.tile([P, E2], U8, align_bytes=64)
+            nc.vector.quantize_mx(out=x_codes[:].bitcast(FP8X4), scales=x_scales[:], in_=x_grouped[:])
+            nc.vector.quantize_mx(out=w_codes[:].bitcast(FP8X4), scales=w_scales[:], in_=w_grouped[:])
+        multiply(PASSES - 1, x_codes, x_scales, w_codes, w_scales)
+
+        capped = tail.tile([P, ROWS, N], F32)
+        expd = tail.tile([P, ROWS, N], F32)
+        logd = tail.tile([P, ROWS, N], F32)
+        en2 = tail.tile([P, ROWS, N], BF16)
+        for j in range(ROWS):
+            nc.vector.tensor_scalar(
+                out=capped[:, j, :], in0=acc[j][:], scalar1=b2_f32[:, j : j + 1], scalar2=EXP_CAP,
+                op0=ALU.add, op1=ALU.min,
+            )
+            nc.scalar.activation(out=expd[:, j, :], in_=capped[:, j, :], func=ACT.Exp)
+        for j in range(ROWS):
+            nc.scalar.activation(out=logd[:, j, :], in_=expd[:, j, :], func=ACT.Ln, bias=1.0)
+            nc.vector.scalar_tensor_tensor(
+                out=en2[:, j, :], in0=acc[j][:], scalar=b2_f32[:, j : j + 1], in1=logd[:, j, :],
+                op0=ALU.add, op1=ALU.max,
+            )
+        nc.scalar.activation(out=warm_out[:], in_=warm_in[:], func=ACT.Exp)
+
+        en2_grouped = tail.tile([P, N, ROWS], BF16, align_bytes=64)
+        nc.vector.tensor_copy(out=en2_grouped[:], in_=en2[:].rearrange("p j n -> p n j"))
+        en2_codes = tail.tile([P, N], U32, align_bytes=64)
+        en2_scales = tail.tile([P, N], U8, align_bytes=64)
+        nc.vector.quantize_mx(
+            out=en2_codes[:].bitcast(FP8X4), scales=en2_scales[:],
+            in_=en2_grouped[:].rearrange("p n j -> p (n j)"),
+        )
+        heads = []
+        for w in range(2):
+            head = psum.tile([P, N], F32, tag="bank", name="head")
+            cols = slice(C * w, C * (w + 1))
+            nc.tensor.matmul_mx(
+                out=head[:],
+                lhsT=wmv_codes[:, cols].bitcast(FP8X4),
+                lhsT_scale=wmv_scales[:, cols],
+                rhs=en2_codes[:].bitcast(FP8X4),
+                rhs_scale=en2_scales[:],
+                start=True,
+                stop=True,
+            )
+            heads.append(head)
+
+        stats = tail.tile([P, 2, 6], F32)
+        mean_var = tail.tile([P, 2, 2], F32)
+        for w in range(2):
+            nc.vector.bn_stats(out=stats[:, w, :], in_=heads[w][:])
+            nc.vector.bn_aggr(out=mean_var[:, w, :], in_=stats[:, w, :])
+        var_eps = tail.tile([P, 2], F32)
+        nc.vector.tensor_scalar(out=var_eps[:], in0=mean_var[:, :, 1], scalar1=BN_EPS, scalar2=None, op0=ALU.add)
+        rstd = tail.tile([P, 2], F32)
+        nc.gpsimd.tensor_tensor(out=rstd[:], in0=var_eps[:], in1=neg_half[:], op=ALU.pow)
+        scale = tail.tile([P, 2], F32)
+        shift = tail.tile([P, 2], F32)
+        nc.vector.tensor_tensor(out=scale[:], in0=rstd[:], in1=gamma[:], op=ALU.mult)
+        nc.vector.tensor_tensor(out=shift[:], in0=mean_var[:, :, 0], in1=scale[:], op=ALU.mult)
+        nc.vector.tensor_tensor(out=shift[:], in0=beta[:], in1=shift[:], op=ALU.subtract)
+
+        std = tail.tile([P, N], F32)
+        nc.scalar.activation(out=std[:], in_=heads[1][:], func=ACT.Exp, bias=shift[:, 1:2], scale=scale[:, 1:2])
+        z_t = tail.tile([P, N], F32)
+        nc.vector.tensor_scalar(
+            out=z_t[:], in0=heads[0][:], scalar1=scale[:, 0:1], scalar2=shift[:, 0:1], op0=ALU.mult, op1=ALU.add
+        )
+        noise = tail.tile([P, N], F32)
+        nc.vector.tensor_tensor(out=noise[:], in0=std[:], in1=eps_t[:].rearrange("c i p -> c (i p)"), op=ALU.mult)
+        nc.vector.tensor_tensor(out=z_t[:], in0=z_t[:], in1=noise[:], op=ALU.add)
+
+        z_bank = psum.tile([P, ROWS, C], F32, tag="bank", name="z_bank")
+        for i in range(ROWS):
+            nc.tensor.transpose(z_bank[:, i, :], z_t[:, P * i : P * (i + 1)], ident[:])
+        z = tail.tile([P, ROWS, C], F32)
+        nc.vector.tensor_copy(out=z[:], in_=z_bank[:])
+        nc.sync.dma_start(out=out.rearrange("(p i) c -> p i c", i=ROWS), in_=z[:])

@@ -23,7 +23,7 @@ WORDS = K_PASS // 2
 CHUNK_PASSES = 2
 CHUNK = CHUNK_PASSES * K_PASS
 BN_EPS = 1e-5
-EXP_CAP = 30.0
+EXP_CAP = 1.0e13
 
 FLOPS = 2 * N * E1 * E2 + 2 * 2 * N * E2 * C
 
@@ -170,34 +170,40 @@ def tile_model_pa_k_kernel(tc, en1, eps, W2, b2, Wm, Wv, gm, betam, gv, betav, o
             nc.vector.quantize_mx(out=w_codes[:].bitcast(FP8X4), scales=w_scales[:], in_=w_grouped[:])
         multiply(PASSES - 1, x_codes, x_scales, w_codes, w_scales)
 
-        capped = tail.tile([P, ROWS, N], F32)
         expd = tail.tile([P, ROWS, N], F32)
-        logd = tail.tile([P, ROWS, N], F32)
-        en2 = tail.tile([P, ROWS, N], BF16)
+        capped = tail.tile([P, ROWS, N], F32)
+        pre = tail.tile([P, ROWS, N], BF16)
+        logd = tail.tile([P, ROWS, N], BF16)
         for j in range(ROWS):
-            nc.vector.tensor_scalar(
-                out=capped[:, j, :], in0=acc[j][:], scalar1=b2_f32[:, j : j + 1], scalar2=EXP_CAP,
-                op0=ALU.add, op1=ALU.min,
-            )
-            nc.scalar.activation(out=expd[:, j, :], in_=capped[:, j, :], func=ACT.Exp)
-        for j in range(ROWS):
-            nc.scalar.activation(out=logd[:, j, :], in_=expd[:, j, :], func=ACT.Ln, bias=1.0)
-            nc.vector.scalar_tensor_tensor(
-                out=en2[:, j, :], in0=acc[j][:], scalar=b2_f32[:, j : j + 1], in1=logd[:, j, :],
-                op0=ALU.add, op1=ALU.max,
-            )
-        nc.scalar.activation(out=warm_out[:], in_=warm_in[:], func=ACT.Exp)
+            bias = b2_f32[:, j : j + 1]
+            nc.scalar.activation(out=expd[:, j, :], in_=acc[j][:], func=ACT.Exp, bias=bias)
+            nc.vector.tensor_scalar(out=pre[:, j, :], in0=acc[j][:], scalar1=bias, scalar2=None, op0=ALU.add)
+            nc.vector.tensor_scalar(out=capped[:, j, :], in0=expd[:, j, :], scalar1=EXP_CAP, scalar2=None, op0=ALU.min)
 
+        halves = [slice(0, N // 2), slice(N // 2, N)]
+        en2 = tail.tile([P, ROWS, N], BF16)
         en2_grouped = tail.tile([P, N, ROWS], BF16, align_bytes=64)
-        nc.vector.tensor_copy(out=en2_grouped[:], in_=en2[:].rearrange("p j n -> p n j"))
         en2_codes = tail.tile([P, N], U32, align_bytes=64)
         en2_scales = tail.tile([P, N], U8, align_bytes=64)
-        nc.vector.quantize_mx(
-            out=en2_codes[:].bitcast(FP8X4), scales=en2_scales[:],
-            in_=en2_grouped[:].rearrange("p n j -> p (n j)"),
-        )
-        heads = []
-        for w in range(2):
+
+        def quantize_half(cols):
+            nc.vector.quantize_mx(
+                out=en2_codes[:, cols].bitcast(FP8X4), scales=en2_scales[:, cols],
+                in_=en2_grouped[:, cols, :].rearrange("p n j -> p (n j)"),
+            )
+
+        for h, cols in enumerate(halves):
+            for j in range(ROWS):
+                nc.scalar.activation(out=logd[:, j, cols], in_=capped[:, j, cols], func=ACT.Ln, bias=1.0)
+            nc.vector.tensor_tensor(out=en2[:, :, cols], in0=pre[:, :, cols], in1=logd[:, :, cols], op=ALU.max)
+            if h == 1:
+                quantize_half(halves[0])
+            nc.vector.tensor_copy(out=en2_grouped[:, cols, :], in_=en2[:, :, cols].rearrange("p j n -> p n j"))
+        quantize_half(halves[1])
+        nc.scalar.activation(out=warm_out[:], in_=warm_in[:], func=ACT.Exp)
+
+        heads = [None, None]
+        for w in (1, 0):
             head = psum.tile([P, N], F32, tag="bank", name="head")
             cols = slice(C * w, C * (w + 1))
             nc.tensor.matmul_mx(
@@ -209,36 +215,55 @@ def tile_model_pa_k_kernel(tc, en1, eps, W2, b2, Wm, Wv, gm, betam, gv, betav, o
                 start=True,
                 stop=True,
             )
-            heads.append(head)
+            heads[w] = head
 
         stats = tail.tile([P, 2, 6], F32)
         mean_var = tail.tile([P, 2, 2], F32)
-        for w in range(2):
+        for w in (1, 0):
             nc.vector.bn_stats(out=stats[:, w, :], in_=heads[w][:])
+        for w in (1, 0):
             nc.vector.bn_aggr(out=mean_var[:, w, :], in_=stats[:, w, :])
         var_eps = tail.tile([P, 2], F32)
         nc.vector.tensor_scalar(out=var_eps[:], in0=mean_var[:, :, 1], scalar1=BN_EPS, scalar2=None, op0=ALU.add)
         rstd = tail.tile([P, 2], F32)
         nc.gpsimd.tensor_tensor(out=rstd[:], in0=var_eps[:], in1=neg_half[:], op=ALU.pow)
+        neg_mean_gamma = tail.tile([P, 2], F32)
+        nc.vector.scalar_tensor_tensor(
+            out=neg_mean_gamma[:], in0=mean_var[:, :, 0], scalar=-1.0, in1=gamma[:], op0=ALU.mult, op1=ALU.mult
+        )
         scale = tail.tile([P, 2], F32)
-        shift = tail.tile([P, 2], F32)
         nc.vector.tensor_tensor(out=scale[:], in0=rstd[:], in1=gamma[:], op=ALU.mult)
-        nc.vector.tensor_tensor(out=shift[:], in0=mean_var[:, :, 0], in1=scale[:], op=ALU.mult)
-        nc.vector.tensor_tensor(out=shift[:], in0=beta[:], in1=shift[:], op=ALU.subtract)
+        shift = tail.tile([P, 2], F32)
+        for w in (1, 0):
+            one = slice(w, w + 1)
+            nc.vector.scalar_tensor_tensor(
+                out=shift[:, one], in0=rstd[:, one], scalar=neg_mean_gamma[:, one], in1=beta[:, one],
+                op0=ALU.mult, op1=ALU.add,
+            )
 
         std = tail.tile([P, N], F32)
-        nc.scalar.activation(out=std[:], in_=heads[1][:], func=ACT.Exp, bias=shift[:, 1:2], scale=scale[:, 1:2])
-        z_t = tail.tile([P, N], F32)
-        nc.vector.tensor_scalar(
-            out=z_t[:], in0=heads[0][:], scalar1=scale[:, 0:1], scalar2=shift[:, 0:1], op0=ALU.mult, op1=ALU.add
-        )
         noise = tail.tile([P, N], F32)
-        nc.vector.tensor_tensor(out=noise[:], in0=std[:], in1=eps_t[:].rearrange("c i p -> c (i p)"), op=ALU.mult)
-        nc.vector.tensor_tensor(out=z_t[:], in0=z_t[:], in1=noise[:], op=ALU.add)
+        mean = tail.tile([P, N], F32)
+        z_t = tail.tile([P, N], F32)
+        eps_cols = eps_t[:].rearrange("c i p -> c (i p)")
+        for cols in halves:
+            nc.scalar.activation(
+                out=std[:, cols], in_=heads[1][:, cols], func=ACT.Exp, bias=shift[:, 1:2], scale=scale[:, 1:2]
+            )
+        nc.vector.tensor_scalar(
+            out=mean[:], in0=heads[0][:], scalar1=scale[:, 0:1], scalar2=shift[:, 0:1], op0=ALU.mult, op1=ALU.add
+        )
+        for cols in halves:
+            nc.vector.tensor_tensor(out=noise[:, cols], in0=std[:, cols], in1=eps_cols[:, cols], op=ALU.mult)
+        for cols in halves:
+            nc.vector.tensor_tensor(out=z_t[:, cols], in0=mean[:, cols], in1=noise[:, cols], op=ALU.add)
 
-        z_bank = psum.tile([P, ROWS, C], F32, tag="bank", name="z_bank")
-        for i in range(ROWS):
-            nc.tensor.transpose(z_bank[:, i, :], z_t[:, P * i : P * (i + 1)], ident[:])
-        z = tail.tile([P, ROWS, C], F32)
-        nc.vector.tensor_copy(out=z[:], in_=z_bank[:])
-        nc.sync.dma_start(out=out.rearrange("(p i) c -> p i c", i=ROWS), in_=z[:])
+        out_rows = out.rearrange("(p i) c -> p i c", i=ROWS)
+        for h, (copy, dma) in enumerate(((nc.scalar.copy, nc.scalar.dma_start), (nc.vector.tensor_copy, nc.sync.dma_start))):
+            z_bank = psum.tile([P, 2, C], F32, tag="bank", name="z_bank")
+            for s in range(2):
+                i = 2 * h + s
+                nc.tensor.transpose(z_bank[:, s, :], z_t[:, P * i : P * (i + 1)], ident[:])
+            z = tail.tile([P, 2, C], F32, name="z%d" % h)
+            copy(out=z[:], in_=z_bank[:])
+            dma(out=out_rows[:, 2 * h : 2 * h + 2, :], in_=z[:])

@@ -20,24 +20,22 @@ K_PASS = 512
 PASSES = E1 // K_PASS
 ROWS = 4
 WORDS = K_PASS // 2
-CHUNK_PASSES = 2
-CHUNK = CHUNK_PASSES * K_PASS
+ROUNDS = [1, 1] + [2] * ((PASSES - 2) // 2)
+MAX_CHUNK = 2 * K_PASS
+SMALL_LOADS_AFTER = 2
 BN_EPS = 1e-5
 EXP_CAP = 1.0e13
 
 FLOPS = 2 * N * E1 * E2 + 2 * 2 * N * E2 * C
 
 
-def transpose_pass(nc, psum, words, first_word, ident):
-    banks = []
-    for b in range(2):
-        bank = psum.tile([P, 2, 2, P], F32, tag="bank", name="bank")
-        for s in range(2):
-            for u in range(2):
-                start = first_word + P * u
-                nc.tensor.transpose(bank[:, s, u, :], words[:, 2 * b + s, start : start + P], ident[:])
-        banks.append(bank)
-    return banks
+def transpose_bank(nc, psum, words, first_word, b, ident):
+    bank = psum.tile([P, 2, 2, P], F32, tag="bank", name="bank")
+    for s in range(2):
+        for u in range(2):
+            start = first_word + P * u
+            nc.tensor.transpose(bank[:, s, u, :], words[:, 2 * b + s, start : start + P], ident[:])
+    return bank
 
 
 def bank_to_grouped(copy, grouped, b, bank):
@@ -54,7 +52,7 @@ def tile_model_pa_k_kernel(tc, en1, eps, W2, b2, Wm, Wv, gm, betam, gv, betav, o
         ctx.enter_context(tc.manual_schedule())
         const = ctx.enter_context(tc.tile_pool(name="const", bufs=1))
         raw = ctx.enter_context(tc.tile_pool(name="raw", bufs=4))
-        stage = ctx.enter_context(tc.tile_pool(name="stage", bufs=3))
+        stage = ctx.enter_context(tc.tile_pool(name="stage", bufs=4))
         tail = ctx.enter_context(tc.tile_pool(name="tail", bufs=1))
         psum_acc = ctx.enter_context(tc.psum_pool(name="psum_acc", bufs=1))
         psum = ctx.enter_context(tc.psum_pool(name="psum", bufs=4))
@@ -62,14 +60,10 @@ def tile_model_pa_k_kernel(tc, en1, eps, W2, b2, Wm, Wv, gm, betam, gv, betav, o
         en1_rows = en1.rearrange("(p i) k -> p i k", i=ROWS)
         w2_rows = W2.rearrange("(p i) k -> p i k", i=ROWS)
 
-        wmv_raw = const.tile([P, 2, E2], BF16)
-        nc.scalar.dma_start(out=wmv_raw[:, 0, :], in_=Wm)
-        nc.scalar.dma_start(out=wmv_raw[:, 1, :], in_=Wv)
-        eps_raw = const.tile([P, ROWS, C], BF16)
-        nc.scalar.dma_start(out=eps_raw[:], in_=eps.rearrange("(p i) c -> p i c", i=ROWS))
-
         ident = const.tile([P, P], F32)
         make_identity(nc, ident[:])
+        ident_bf16 = const.tile([P, P], BF16)
+        nc.vector.tensor_copy(out=ident_bf16[:], in_=ident[:])
 
         b2_raw = const.tile([P, ROWS], BF16)
         gm_raw = const.tile([P, 1], BF16)
@@ -101,74 +95,62 @@ def tile_model_pa_k_kernel(tc, en1, eps, W2, b2, Wm, Wv, gm, betam, gv, betav, o
         neg_half = const.tile([P, 2], F32)
         nc.vector.memset(neg_half[:], -0.5)
 
-        eps_f32 = const.tile([P, ROWS, C], F32)
-        nc.vector.tensor_copy(out=eps_f32[:], in_=eps_raw[:])
-
-        wmv_words = wmv_raw[:].bitcast(F32).rearrange("c w (p u) -> c w u p", u=2)
-        wmv_bank = psum.tile([P, 2, 2, P], F32, tag="bank", name="wmv_bank")
-        for w in range(2):
-            for u in range(2):
-                nc.tensor.transpose(wmv_bank[:, w, u, :], wmv_words[:, w, u, :], ident[:])
-        wmv_grouped = const.tile([P, 2 * C * 4], BF16, align_bytes=64)
-        nc.vector.tensor_copy(
-            out=wmv_grouped[:].bitcast(F32).rearrange("q (w c u) -> q w c u", w=2, u=2),
-            in_=wmv_bank[:].rearrange("q w u c -> q w c u"),
-        )
-
-        eps_bank = psum.tile([P, ROWS, P], F32, tag="bank", name="eps_bank")
-        for i in range(ROWS):
-            nc.tensor.transpose(eps_bank[:, i, :], eps_f32[:, i, :], ident[:])
-        eps_t = const.tile([P, ROWS, P], F32)
-        nc.scalar.copy(out=eps_t[:], in_=eps_bank[:])
-
-        wmv_codes = const.tile([P, 2 * C], U32, align_bytes=64)
-        wmv_scales = const.tile([P, 2 * C], U8, align_bytes=64)
-        nc.vector.quantize_mx(out=wmv_codes[:].bitcast(FP8X4), scales=wmv_scales[:], in_=wmv_grouped[:])
-
+        wmv_raw = const.tile([P, 2, E2], BF16)
+        eps_raw = const.tile([P, ROWS, C], BF16)
 
         acc = [psum_acc.tile([P, N], F32, name="acc%d" % j) for j in range(ROWS)]
 
-        def multiply(g, x_codes, x_scales, w_codes, w_scales):
+        def multiply(operands, start, stop):
             for j in range(ROWS):
                 cols = slice(P * j, P * (j + 1))
-                nc.tensor.matmul_mx(
-                    out=acc[j][:],
-                    lhsT=w_codes[:, cols].bitcast(FP8X4),
-                    lhsT_scale=w_scales[:, cols],
-                    rhs=x_codes[:].bitcast(FP8X4),
-                    rhs_scale=x_scales[:],
-                    start=(g == 0),
-                    stop=(g == PASSES - 1),
-                )
+                for t, (x_codes, x_scales, w_codes, w_scales) in enumerate(operands):
+                    nc.tensor.matmul_mx(
+                        out=acc[j][:],
+                        lhsT=w_codes[:, cols].bitcast(FP8X4),
+                        lhsT_scale=w_scales[:, cols],
+                        rhs=x_codes[:].bitcast(FP8X4),
+                        rhs_scale=x_scales[:],
+                        start=(start and t == 0),
+                        stop=(stop and t == len(operands) - 1),
+                    )
 
-        for g in range(PASSES):
-            if g % CHUNK_PASSES == 0:
-                k_cols = slice(K_PASS * g, K_PASS * g + CHUNK)
-                x_raw = raw.tile([P, ROWS, CHUNK], BF16)
-                nc.sync.dma_start(out=x_raw[:], in_=en1_rows[:, :, k_cols])
-                w_raw = raw.tile([P, ROWS, CHUNK], BF16)
-                nc.sync.dma_start(out=w_raw[:], in_=w2_rows[:, :, k_cols])
-            first_word = WORDS * (g % CHUNK_PASSES)
+        before = []
+        first_pass = 0
+        for r, passes in enumerate(ROUNDS):
+            k_cols = slice(K_PASS * first_pass, K_PASS * (first_pass + passes))
+            x_raw = raw.tile([P, ROWS, MAX_CHUNK], BF16)
+            nc.sync.dma_start(out=x_raw[:, :, : K_PASS * passes], in_=en1_rows[:, :, k_cols])
+            w_raw = raw.tile([P, ROWS, MAX_CHUNK], BF16)
+            nc.sync.dma_start(out=w_raw[:, :, : K_PASS * passes], in_=w2_rows[:, :, k_cols])
+            if r == SMALL_LOADS_AFTER:
+                nc.sync.dma_start(out=wmv_raw[:, 0, :], in_=Wm)
+                nc.sync.dma_start(out=wmv_raw[:, 1, :], in_=Wv)
+                nc.sync.dma_start(out=eps_raw[:], in_=eps.rearrange("(p i) c -> p i c", i=ROWS))
 
-            x_banks = transpose_pass(nc, psum, x_raw[:].bitcast(F32), first_word, ident)
-            w_banks = transpose_pass(nc, psum, w_raw[:].bitcast(F32), first_word, ident)
-            if g > 0:
-                multiply(g - 1, x_codes, x_scales, w_codes, w_scales)
+            grouped = []
+            bank_number = 0
+            for t in range(passes):
+                for words, name in ((x_raw, "x_grouped"), (w_raw, "w_grouped")):
+                    tile = stage.tile([P, 4 * N], BF16, align_bytes=64, name=name)
+                    for b in range(2):
+                        bank = transpose_bank(nc, psum, words[:].bitcast(F32), WORDS * t, b, ident)
+                        copy = nc.vector.tensor_copy if bank_number in (1, 3) else nc.scalar.copy
+                        bank_to_grouped(copy, tile, b, bank)
+                        bank_number += 1
+                    grouped.append(tile)
+            multiply(before, start=(r == 1), stop=False)
 
-            x_grouped = stage.tile([P, 4 * N], BF16, align_bytes=64)
-            w_grouped = stage.tile([P, 4 * E2], BF16, align_bytes=64)
-            bank_to_grouped(nc.scalar.copy, x_grouped, 0, x_banks[0])
-            bank_to_grouped(nc.scalar.copy, x_grouped, 1, x_banks[1])
-            bank_to_grouped(nc.scalar.copy, w_grouped, 0, w_banks[0])
-            bank_to_grouped(nc.vector.tensor_copy, w_grouped, 1, w_banks[1])
-
-            x_codes = stage.tile([P, N], U32, align_bytes=64)
-            x_scales = stage.tile([P, N], U8, align_bytes=64)
-            w_codes = stage.tile([P, E2], U32, align_bytes=64)
-            w_scales = stage.tile([P, E2], U8, align_bytes=64)
-            nc.vector.quantize_mx(out=x_codes[:].bitcast(FP8X4), scales=x_scales[:], in_=x_grouped[:])
-            nc.vector.quantize_mx(out=w_codes[:].bitcast(FP8X4), scales=w_scales[:], in_=w_grouped[:])
-        multiply(PASSES - 1, x_codes, x_scales, w_codes, w_scales)
+            before = []
+            for t in range(passes):
+                x_codes = stage.tile([P, N], U32, align_bytes=64)
+                x_scales = stage.tile([P, N], U8, align_bytes=64)
+                w_codes = stage.tile([P, E2], U32, align_bytes=64)
+                w_scales = stage.tile([P, E2], U8, align_bytes=64)
+                nc.vector.quantize_mx(out=x_codes[:].bitcast(FP8X4), scales=x_scales[:], in_=grouped[2 * t][:])
+                nc.vector.quantize_mx(out=w_codes[:].bitcast(FP8X4), scales=w_scales[:], in_=grouped[2 * t + 1][:])
+                before.append((x_codes, x_scales, w_codes, w_scales))
+            first_pass += passes
+        multiply(before, start=False, stop=True)
 
         expd = tail.tile([P, ROWS, N], F32)
         capped = tail.tile([P, ROWS, N], F32)
@@ -179,6 +161,23 @@ def tile_model_pa_k_kernel(tc, en1, eps, W2, b2, Wm, Wv, gm, betam, gv, betav, o
             nc.scalar.activation(out=expd[:, j, :], in_=acc[j][:], func=ACT.Exp, bias=bias)
             nc.vector.tensor_scalar(out=pre[:, j, :], in0=acc[j][:], scalar1=bias, scalar2=None, op0=ALU.add)
             nc.vector.tensor_scalar(out=capped[:, j, :], in0=expd[:, j, :], scalar1=EXP_CAP, scalar2=None, op0=ALU.min)
+
+        wmv_words = wmv_raw[:].bitcast(F32).rearrange("c w (p u) -> c w u p", u=2)
+        wmv_bank = psum.tile([P, 2, 2, P], F32, tag="bank", name="wmv_bank")
+        for w in range(2):
+            for u in range(2):
+                nc.tensor.transpose(wmv_bank[:, w, u, :], wmv_words[:, w, u, :], ident[:])
+        eps_bank = psum.tile([P, ROWS, P], BF16, tag="bank", name="eps_bank")
+        for i in range(ROWS):
+            nc.tensor.transpose(eps_bank[:, i, :], eps_raw[:, i, :], ident_bf16[:])
+        wmv_grouped = const.tile([P, 2 * C * 4], BF16, align_bytes=64)
+        nc.vector.tensor_copy(
+            out=wmv_grouped[:].bitcast(F32).rearrange("q (w c u) -> q w c u", w=2, u=2),
+            in_=wmv_bank[:].rearrange("q w u c -> q w c u"),
+        )
+        wmv_codes = const.tile([P, 2 * C], U32, align_bytes=64)
+        wmv_scales = const.tile([P, 2 * C], U8, align_bytes=64)
+        nc.vector.quantize_mx(out=wmv_codes[:].bitcast(FP8X4), scales=wmv_scales[:], in_=wmv_grouped[:])
 
         halves = [slice(0, N // 2), slice(N // 2, N)]
         en2 = tail.tile([P, ROWS, N], BF16)
@@ -201,6 +200,8 @@ def tile_model_pa_k_kernel(tc, en1, eps, W2, b2, Wm, Wv, gm, betam, gv, betav, o
             nc.vector.tensor_copy(out=en2_grouped[:, cols, :], in_=en2[:, :, cols].rearrange("p j n -> p n j"))
         quantize_half(halves[1])
         nc.scalar.activation(out=warm_out[:], in_=warm_in[:], func=ACT.Exp)
+        eps_t = const.tile([P, ROWS, P], F32)
+        nc.scalar.copy(out=eps_t[:], in_=eps_bank[:])
 
         heads = [None, None]
         for w in (1, 0):

@@ -20,8 +20,8 @@ K_PASS = 512
 PASSES = E1 // K_PASS
 ROWS = 4
 WORDS = K_PASS // 2
-ROUNDS = [1, 1] + [2] * ((PASSES - 2) // 2)
-MAX_CHUNK = 2 * K_PASS
+LOADS = [1, 1] + [2] * ((PASSES - 2) // 2)
+MAX_LOAD = 2 * K_PASS
 SMALL_LOADS_AFTER = 2
 BN_EPS = 1e-5
 EXP_CAP = 1.0e13
@@ -52,7 +52,7 @@ def tile_model_pa_k_kernel(tc, en1, eps, W2, b2, Wm, Wv, gm, betam, gv, betav, o
         ctx.enter_context(tc.manual_schedule())
         const = ctx.enter_context(tc.tile_pool(name="const", bufs=1))
         raw = ctx.enter_context(tc.tile_pool(name="raw", bufs=4))
-        stage = ctx.enter_context(tc.tile_pool(name="stage", bufs=4))
+        stage = ctx.enter_context(tc.tile_pool(name="stage", bufs=3))
         tail = ctx.enter_context(tc.tile_pool(name="tail", bufs=1))
         psum_acc = ctx.enter_context(tc.psum_pool(name="psum_acc", bufs=1))
         psum = ctx.enter_context(tc.psum_pool(name="psum", bufs=4))
@@ -100,57 +100,52 @@ def tile_model_pa_k_kernel(tc, en1, eps, W2, b2, Wm, Wv, gm, betam, gv, betav, o
 
         acc = [psum_acc.tile([P, N], F32, name="acc%d" % j) for j in range(ROWS)]
 
-        def multiply(operands, start, stop):
+        def multiply(g, x_codes, x_scales, w_codes, w_scales):
             for j in range(ROWS):
                 cols = slice(P * j, P * (j + 1))
-                for t, (x_codes, x_scales, w_codes, w_scales) in enumerate(operands):
-                    nc.tensor.matmul_mx(
-                        out=acc[j][:],
-                        lhsT=w_codes[:, cols].bitcast(FP8X4),
-                        lhsT_scale=w_scales[:, cols],
-                        rhs=x_codes[:].bitcast(FP8X4),
-                        rhs_scale=x_scales[:],
-                        start=(start and t == 0),
-                        stop=(stop and t == len(operands) - 1),
-                    )
+                nc.tensor.matmul_mx(
+                    out=acc[j][:],
+                    lhsT=w_codes[:, cols].bitcast(FP8X4),
+                    lhsT_scale=w_scales[:, cols],
+                    rhs=x_codes[:].bitcast(FP8X4),
+                    rhs_scale=x_scales[:],
+                    start=(g == 0),
+                    stop=(g == PASSES - 1),
+                )
 
-        before = []
-        first_pass = 0
-        for r, passes in enumerate(ROUNDS):
-            k_cols = slice(K_PASS * first_pass, K_PASS * (first_pass + passes))
-            x_raw = raw.tile([P, ROWS, MAX_CHUNK], BF16)
+        g = 0
+        for load, passes in enumerate(LOADS):
+            k_cols = slice(K_PASS * g, K_PASS * (g + passes))
+            x_raw = raw.tile([P, ROWS, MAX_LOAD], BF16)
             nc.sync.dma_start(out=x_raw[:, :, : K_PASS * passes], in_=en1_rows[:, :, k_cols])
-            w_raw = raw.tile([P, ROWS, MAX_CHUNK], BF16)
+            w_raw = raw.tile([P, ROWS, MAX_LOAD], BF16)
             nc.sync.dma_start(out=w_raw[:, :, : K_PASS * passes], in_=w2_rows[:, :, k_cols])
-            if r == SMALL_LOADS_AFTER:
+            if load == SMALL_LOADS_AFTER:
                 nc.sync.dma_start(out=wmv_raw[:, 0, :], in_=Wm)
                 nc.sync.dma_start(out=wmv_raw[:, 1, :], in_=Wv)
                 nc.sync.dma_start(out=eps_raw[:], in_=eps.rearrange("(p i) c -> p i c", i=ROWS))
 
-            grouped = []
-            bank_number = 0
             for t in range(passes):
-                for words, name in ((x_raw, "x_grouped"), (w_raw, "w_grouped")):
-                    tile = stage.tile([P, 4 * N], BF16, align_bytes=64, name=name)
-                    for b in range(2):
-                        bank = transpose_bank(nc, psum, words[:].bitcast(F32), WORDS * t, b, ident)
-                        copy = nc.vector.tensor_copy if bank_number in (1, 3) else nc.scalar.copy
-                        bank_to_grouped(copy, tile, b, bank)
-                        bank_number += 1
-                    grouped.append(tile)
-            multiply(before, start=(r == 1), stop=False)
+                x_banks = [transpose_bank(nc, psum, x_raw[:].bitcast(F32), WORDS * t, b, ident) for b in range(2)]
+                w_banks = [transpose_bank(nc, psum, w_raw[:].bitcast(F32), WORDS * t, b, ident) for b in range(2)]
+                if g > 0:
+                    multiply(g - 1, x_codes, x_scales, w_codes, w_scales)
 
-            before = []
-            for t in range(passes):
+                x_grouped = stage.tile([P, 4 * N], BF16, align_bytes=64)
+                w_grouped = stage.tile([P, 4 * E2], BF16, align_bytes=64)
+                bank_to_grouped(nc.scalar.copy, x_grouped, 0, x_banks[0])
+                bank_to_grouped(nc.scalar.copy, x_grouped, 1, x_banks[1])
+                bank_to_grouped(nc.scalar.copy, w_grouped, 0, w_banks[0])
+                bank_to_grouped(nc.vector.tensor_copy, w_grouped, 1, w_banks[1])
+
                 x_codes = stage.tile([P, N], U32, align_bytes=64)
                 x_scales = stage.tile([P, N], U8, align_bytes=64)
                 w_codes = stage.tile([P, E2], U32, align_bytes=64)
                 w_scales = stage.tile([P, E2], U8, align_bytes=64)
-                nc.vector.quantize_mx(out=x_codes[:].bitcast(FP8X4), scales=x_scales[:], in_=grouped[2 * t][:])
-                nc.vector.quantize_mx(out=w_codes[:].bitcast(FP8X4), scales=w_scales[:], in_=grouped[2 * t + 1][:])
-                before.append((x_codes, x_scales, w_codes, w_scales))
-            first_pass += passes
-        multiply(before, start=False, stop=True)
+                nc.vector.quantize_mx(out=x_codes[:].bitcast(FP8X4), scales=x_scales[:], in_=x_grouped[:])
+                nc.vector.quantize_mx(out=w_codes[:].bitcast(FP8X4), scales=w_scales[:], in_=w_grouped[:])
+                g += 1
+        multiply(PASSES - 1, x_codes, x_scales, w_codes, w_scales)
 
         expd = tail.tile([P, ROWS, N], F32)
         capped = tail.tile([P, ROWS, N], F32)

@@ -22,7 +22,7 @@ ROWS = 4
 WORDS = K_PASS // 2
 LOADS = [1, 1] + [2] * ((PASSES - 2) // 2)
 MAX_LOAD = 2 * K_PASS
-SMALL_LOADS_AFTER = 2
+RAW_BUFS = 4
 BN_EPS = 1e-5
 EXP_CAP = 1.0e13
 
@@ -51,7 +51,7 @@ def tile_model_pa_k_kernel(tc, en1, eps, W2, b2, Wm, Wv, gm, betam, gv, betav, o
     with ExitStack() as ctx:
         ctx.enter_context(tc.manual_schedule())
         const = ctx.enter_context(tc.tile_pool(name="const", bufs=1))
-        raw = ctx.enter_context(tc.tile_pool(name="raw", bufs=4))
+        raw = ctx.enter_context(tc.tile_pool(name="raw", bufs=RAW_BUFS))
         stage = ctx.enter_context(tc.tile_pool(name="stage", bufs=3))
         tail = ctx.enter_context(tc.tile_pool(name="tail", bufs=1))
         psum_acc = ctx.enter_context(tc.psum_pool(name="psum_acc", bufs=1))
@@ -60,40 +60,32 @@ def tile_model_pa_k_kernel(tc, en1, eps, W2, b2, Wm, Wv, gm, betam, gv, betav, o
         en1_rows = en1.rearrange("(p i) k -> p i k", i=ROWS)
         w2_rows = W2.rearrange("(p i) k -> p i k", i=ROWS)
 
+        rows_raw = const.tile([P, E2], BF16)
+        nc.vector.memset(rows_raw[:], 0.0)
+        nc.scalar.dma_start(out=rows_raw[0:1, :], in_=b2.rearrange("(o k) -> o k", o=1))
+        for i, vec in enumerate((gm, betam, gv, betav)):
+            nc.scalar.dma_start(out=rows_raw[1:2, C * i : C * (i + 1)], in_=vec.rearrange("(o k) -> o k", o=1))
+
         ident = const.tile([P, P], F32)
         make_identity(nc, ident[:])
         ident_bf16 = const.tile([P, P], BF16)
         nc.vector.tensor_copy(out=ident_bf16[:], in_=ident[:])
 
-        b2_raw = const.tile([P, ROWS], BF16)
-        gm_raw = const.tile([P, 1], BF16)
-        gv_raw = const.tile([P, 1], BF16)
-        betam_raw = const.tile([P, 1], BF16)
-        betav_raw = const.tile([P, 1], BF16)
-        with nc.allow_non_contiguous_dma(reason="one or four elements a partition, once"):
-            nc.gpsimd.dma_start(out=b2_raw[:], in_=b2.rearrange("(p i) -> p i", i=ROWS))
-            nc.gpsimd.dma_start(out=gm_raw[:], in_=gm.rearrange("(p o) -> p o", o=1))
-            nc.gpsimd.dma_start(out=gv_raw[:], in_=gv.rearrange("(p o) -> p o", o=1))
-            nc.gpsimd.dma_start(out=betam_raw[:], in_=betam.rearrange("(p o) -> p o", o=1))
-            nc.gpsimd.dma_start(out=betav_raw[:], in_=betav.rearrange("(p o) -> p o", o=1))
+        rows_bank = psum.tile([P, 2, ROWS, P], BF16, tag="bank", name="rows_bank")
+        for i in range(ROWS):
+            nc.tensor.transpose(rows_bank[:, 0, i, :], rows_raw[:, i : E2 : ROWS], ident_bf16[:])
+            nc.tensor.transpose(rows_bank[:, 1, i, :], rows_raw[:, C * i : C * (i + 1)], ident_bf16[:])
         b2_f32 = const.tile([P, ROWS], F32)
-        gamma = const.tile([P, 2], F32)
-        beta = const.tile([P, 2], F32)
-        for dst, src, factor in (
-            (b2_f32[:], b2_raw, 1.0),
-            (gamma[:, 0:1], gm_raw, 1.0),
-            (gamma[:, 1:2], gv_raw, 0.5),
-            (beta[:, 0:1], betam_raw, 1.0),
-            (beta[:, 1:2], betav_raw, 0.5),
-        ):
-            nc.gpsimd.tensor_scalar(out=dst, in0=src[:], scalar1=factor, scalar2=0.0, op0=ALU.mult, op1=ALU.add)
-
-        warm_in = const.tile([P, 1], F32)
-        warm_out = const.tile([P, 1], F32)
-        nc.vector.memset(warm_in[:], 0.0)
-        nc.scalar.activation(out=warm_out[:], in_=warm_in[:], func=ACT.Exp)
-        neg_half = const.tile([P, 2], F32)
-        nc.vector.memset(neg_half[:], -0.5)
+        nc.vector.tensor_copy(out=b2_f32[:], in_=rows_bank[:, 0, :, 0])
+        params = const.tile([P, 2, 2], F32)
+        nc.vector.tensor_scalar(
+            out=params[:, :, 0], in0=rows_bank[:, 1, 0:2, 1], scalar1=1.0, scalar2=None, op0=ALU.mult
+        )
+        nc.vector.tensor_scalar(
+            out=params[:, :, 1], in0=rows_bank[:, 1, 2:4, 1], scalar1=0.5, scalar2=None, op0=ALU.mult
+        )
+        gamma = params[:, 0, :]
+        beta = params[:, 1, :]
 
         wmv_raw = const.tile([P, 2, E2], BF16)
         eps_raw = const.tile([P, ROWS, C], BF16)
@@ -113,18 +105,36 @@ def tile_model_pa_k_kernel(tc, en1, eps, W2, b2, Wm, Wv, gm, betam, gv, betav, o
                     stop=(g == PASSES - 1),
                 )
 
+        first_passes = [sum(LOADS[:n]) for n in range(len(LOADS))]
+        x_raws, w_raws = {}, {}
+
+        def load_x(n):
+            k_cols = slice(K_PASS * first_passes[n], K_PASS * (first_passes[n] + LOADS[n]))
+            x_raws[n] = raw.tile([P, ROWS, MAX_LOAD], BF16, name="x_raw")
+            nc.sync.dma_start(out=x_raws[n][:, :, : K_PASS * LOADS[n]], in_=en1_rows[:, :, k_cols])
+
+        def load_w(n):
+            k_cols = slice(K_PASS * first_passes[n], K_PASS * (first_passes[n] + LOADS[n]))
+            w_raws[n] = raw.tile([P, ROWS, MAX_LOAD], BF16, name="w_raw")
+            nc.scalar.dma_start(out=w_raws[n][:, :, : K_PASS * LOADS[n]], in_=w2_rows[:, :, k_cols])
+
+        for n in range(RAW_BUFS):
+            load_x(n)
+            load_w(n)
+        nc.sync.dma_start(out=wmv_raw[:, 0, :], in_=Wm)
+        nc.sync.dma_start(out=wmv_raw[:, 1, :], in_=Wv)
+        nc.sync.dma_start(out=eps_raw[:], in_=eps.rearrange("(p i) c -> p i c", i=ROWS))
+
+        warm_in = const.tile([P, 1], F32)
+        warm_out = const.tile([P, 1], F32)
+        nc.vector.memset(warm_in[:], 0.0)
+        nc.scalar.activation(out=warm_out[:], in_=warm_in[:], func=ACT.Exp)
+        neg_half = const.tile([P, 2], F32)
+        nc.vector.memset(neg_half[:], -0.5)
+
         g = 0
         for load, passes in enumerate(LOADS):
-            k_cols = slice(K_PASS * g, K_PASS * (g + passes))
-            x_raw = raw.tile([P, ROWS, MAX_LOAD], BF16)
-            nc.sync.dma_start(out=x_raw[:, :, : K_PASS * passes], in_=en1_rows[:, :, k_cols])
-            w_raw = raw.tile([P, ROWS, MAX_LOAD], BF16)
-            nc.sync.dma_start(out=w_raw[:, :, : K_PASS * passes], in_=w2_rows[:, :, k_cols])
-            if load == SMALL_LOADS_AFTER:
-                nc.sync.dma_start(out=wmv_raw[:, 0, :], in_=Wm)
-                nc.sync.dma_start(out=wmv_raw[:, 1, :], in_=Wv)
-                nc.sync.dma_start(out=eps_raw[:], in_=eps.rearrange("(p i) c -> p i c", i=ROWS))
-
+            x_raw, w_raw = x_raws.pop(load), w_raws.pop(load)
             for t in range(passes):
                 x_banks = [transpose_bank(nc, psum, x_raw[:].bitcast(F32), WORDS * t, b, ident) for b in range(2)]
                 w_banks = [transpose_bank(nc, psum, w_raw[:].bitcast(F32), WORDS * t, b, ident) for b in range(2)]
@@ -145,6 +155,10 @@ def tile_model_pa_k_kernel(tc, en1, eps, W2, b2, Wm, Wv, gm, betam, gv, betav, o
                 nc.vector.quantize_mx(out=x_codes[:].bitcast(FP8X4), scales=x_scales[:], in_=x_grouped[:])
                 nc.vector.quantize_mx(out=w_codes[:].bitcast(FP8X4), scales=w_scales[:], in_=w_grouped[:])
                 g += 1
+
+            if load + RAW_BUFS < len(LOADS):
+                load_x(load + RAW_BUFS)
+                load_w(load + RAW_BUFS)
         multiply(PASSES - 1, x_codes, x_scales, w_codes, w_scales)
 
         expd = tail.tile([P, ROWS, N], F32)
@@ -225,10 +239,10 @@ def tile_model_pa_k_kernel(tc, en1, eps, W2, b2, Wm, Wv, gm, betam, gv, betav, o
         nc.gpsimd.tensor_tensor(out=rstd[:], in0=var_eps[:], in1=neg_half[:], op=ALU.pow)
         neg_mean_gamma = tail.tile([P, 2], F32)
         nc.vector.scalar_tensor_tensor(
-            out=neg_mean_gamma[:], in0=mean_var[:, :, 0], scalar=-1.0, in1=gamma[:], op0=ALU.mult, op1=ALU.mult
+            out=neg_mean_gamma[:], in0=mean_var[:, :, 0], scalar=-1.0, in1=gamma, op0=ALU.mult, op1=ALU.mult
         )
         scale = tail.tile([P, 2], F32)
-        nc.vector.tensor_tensor(out=scale[:], in0=rstd[:], in1=gamma[:], op=ALU.mult)
+        nc.vector.tensor_tensor(out=scale[:], in0=rstd[:], in1=gamma, op=ALU.mult)
         shift = tail.tile([P, 2], F32)
         for w in (1, 0):
             one = slice(w, w + 1)

@@ -60,33 +60,19 @@ def tile_model_pa_k_kernel(tc, en1, eps, W2, b2, Wm, Wv, gm, betam, gv, betav, o
         en1_rows = en1.rearrange("(p i) k -> p i k", i=ROWS)
         w2_rows = W2.rearrange("(p i) k -> p i k", i=ROWS)
 
-        rows_raw = const.tile([P, E2], BF16)
-        nc.vector.memset(rows_raw[:], 0.0)
-        nc.scalar.dma_start(out=rows_raw[0:1, :], in_=b2.rearrange("(o k) -> o k", o=1))
-        for i, vec in enumerate((gm, betam, gv, betav)):
-            nc.scalar.dma_start(out=rows_raw[1:2, C * i : C * (i + 1)], in_=vec.rearrange("(o k) -> o k", o=1))
-
         ident = const.tile([P, P], F32)
         make_identity(nc, ident[:])
         ident_bf16 = const.tile([P, P], BF16)
         nc.vector.tensor_copy(out=ident_bf16[:], in_=ident[:])
 
-        rows_bank = psum.tile([P, 2, ROWS, P], BF16, tag="bank", name="rows_bank")
-        for i in range(ROWS):
-            nc.tensor.transpose(rows_bank[:, 0, i, :], rows_raw[:, i : E2 : ROWS], ident_bf16[:])
-            nc.tensor.transpose(rows_bank[:, 1, i, :], rows_raw[:, C * i : C * (i + 1)], ident_bf16[:])
+        b2_raw = const.tile([P, ROWS], BF16)
+        with nc.allow_non_contiguous_dma(reason="four elements a partition, once"):
+            nc.gpsimd.dma_start(out=b2_raw[:], in_=b2.rearrange("(p i) -> p i", i=ROWS))
         b2_f32 = const.tile([P, ROWS], F32)
-        nc.vector.tensor_copy(out=b2_f32[:], in_=rows_bank[:, 0, :, 0])
-        params = const.tile([P, 2, 2], F32)
-        nc.vector.tensor_scalar(
-            out=params[:, :, 0], in0=rows_bank[:, 1, 0:2, 1], scalar1=1.0, scalar2=None, op0=ALU.mult
-        )
-        nc.vector.tensor_scalar(
-            out=params[:, :, 1], in0=rows_bank[:, 1, 2:4, 1], scalar1=0.5, scalar2=None, op0=ALU.mult
-        )
-        gamma = params[:, 0, :]
-        beta = params[:, 1, :]
+        nc.gpsimd.tensor_scalar(out=b2_f32[:], in0=b2_raw[:], scalar1=1.0, scalar2=0.0, op0=ALU.mult, op1=ALU.add)
 
+        rows_raw = const.tile([P, ROWS * C], BF16)
+        nc.vector.memset(rows_raw[:], 0.0)
         wmv_raw = const.tile([P, 2, E2], BF16)
         eps_raw = const.tile([P, ROWS, C], BF16)
 
@@ -121,9 +107,6 @@ def tile_model_pa_k_kernel(tc, en1, eps, W2, b2, Wm, Wv, gm, betam, gv, betav, o
         for n in range(RAW_BUFS):
             load_x(n)
             load_w(n)
-        nc.sync.dma_start(out=wmv_raw[:, 0, :], in_=Wm)
-        nc.sync.dma_start(out=wmv_raw[:, 1, :], in_=Wv)
-        nc.sync.dma_start(out=eps_raw[:], in_=eps.rearrange("(p i) c -> p i c", i=ROWS))
 
         warm_in = const.tile([P, 1], F32)
         warm_out = const.tile([P, 1], F32)
@@ -144,9 +127,9 @@ def tile_model_pa_k_kernel(tc, en1, eps, W2, b2, Wm, Wv, gm, betam, gv, betav, o
                 x_grouped = stage.tile([P, 4 * N], BF16, align_bytes=64)
                 w_grouped = stage.tile([P, 4 * E2], BF16, align_bytes=64)
                 bank_to_grouped(nc.scalar.copy, x_grouped, 0, x_banks[0])
-                bank_to_grouped(nc.scalar.copy, x_grouped, 1, x_banks[1])
+                bank_to_grouped(nc.vector.tensor_copy, x_grouped, 1, x_banks[1])
                 bank_to_grouped(nc.scalar.copy, w_grouped, 0, w_banks[0])
-                bank_to_grouped(nc.vector.tensor_copy, w_grouped, 1, w_banks[1])
+                bank_to_grouped(nc.scalar.copy, w_grouped, 1, w_banks[1])
 
                 x_codes = stage.tile([P, N], U32, align_bytes=64)
                 x_scales = stage.tile([P, N], U8, align_bytes=64)
@@ -159,6 +142,12 @@ def tile_model_pa_k_kernel(tc, en1, eps, W2, b2, Wm, Wv, gm, betam, gv, betav, o
             if load + RAW_BUFS < len(LOADS):
                 load_x(load + RAW_BUFS)
                 load_w(load + RAW_BUFS)
+            elif load + RAW_BUFS == len(LOADS):
+                nc.sync.dma_start(out=wmv_raw[:, 0, :], in_=Wm)
+                nc.sync.dma_start(out=wmv_raw[:, 1, :], in_=Wv)
+                nc.sync.dma_start(out=eps_raw[:], in_=eps.rearrange("(p i) c -> p i c", i=ROWS))
+                for i, vec in enumerate((gm, betam, gv, betav)):
+                    nc.sync.dma_start(out=rows_raw[0:1, C * i : C * (i + 1)], in_=vec.rearrange("(o c) -> o c", o=1))
         multiply(PASSES - 1, x_codes, x_scales, w_codes, w_scales)
 
         expd = tail.tile([P, ROWS, N], F32)
@@ -179,6 +168,9 @@ def tile_model_pa_k_kernel(tc, en1, eps, W2, b2, Wm, Wv, gm, betam, gv, betav, o
         eps_bank = psum.tile([P, ROWS, P], BF16, tag="bank", name="eps_bank")
         for i in range(ROWS):
             nc.tensor.transpose(eps_bank[:, i, :], eps_raw[:, i, :], ident_bf16[:])
+        rows_bank = psum.tile([P, 4, P], BF16, tag="bank", name="rows_bank")
+        for i in range(4):
+            nc.tensor.transpose(rows_bank[:, i, :], rows_raw[:, C * i : C * (i + 1)], ident_bf16[:])
         wmv_grouped = const.tile([P, 2 * C * 4], BF16, align_bytes=64)
         nc.vector.tensor_copy(
             out=wmv_grouped[:].bitcast(F32).rearrange("q (w c u) -> q w c u", w=2, u=2),
@@ -186,6 +178,13 @@ def tile_model_pa_k_kernel(tc, en1, eps, W2, b2, Wm, Wv, gm, betam, gv, betav, o
         )
         wmv_codes = const.tile([P, 2 * C], U32, align_bytes=64)
         wmv_scales = const.tile([P, 2 * C], U8, align_bytes=64)
+        params = const.tile([P, 2, 2], F32)
+        for w, factor in enumerate((1.0, 0.5)):
+            nc.vector.tensor_scalar(
+                out=params[:, :, w], in0=rows_bank[:, 2 * w : 2 * w + 2, 0], scalar1=factor, scalar2=None, op0=ALU.mult
+            )
+        gamma = params[:, 0, :]
+        beta = params[:, 1, :]
         nc.vector.quantize_mx(out=wmv_codes[:].bitcast(FP8X4), scales=wmv_scales[:], in_=wmv_grouped[:])
 
         halves = [slice(0, N // 2), slice(N // 2, N)]
@@ -200,39 +199,47 @@ def tile_model_pa_k_kernel(tc, en1, eps, W2, b2, Wm, Wv, gm, betam, gv, betav, o
                 in_=en2_grouped[:, cols, :].rearrange("p n j -> p (n j)"),
             )
 
+        heads = [{}, {}]
+        stats = tail.tile([P, 2, 2, 6], F32)
+
+        def second_layer_half(h):
+            cols = halves[h]
+            for w in (1, 0):
+                heads[w][h] = psum.tile([P, N // 2], F32, tag="bank", name="head")
+                w_cols = slice(C * w, C * (w + 1))
+                nc.tensor.matmul_mx(
+                    out=heads[w][h][:],
+                    lhsT=wmv_codes[:, w_cols].bitcast(FP8X4),
+                    lhsT_scale=wmv_scales[:, w_cols],
+                    rhs=en2_codes[:, cols].bitcast(FP8X4),
+                    rhs_scale=en2_scales[:, cols],
+                    start=True,
+                    stop=True,
+                )
+
+        def stats_half(h):
+            for w in (1, 0):
+                nc.vector.bn_stats(out=stats[:, w, h, :], in_=heads[w][h][:])
+
         for h, cols in enumerate(halves):
             for j in range(ROWS):
                 nc.scalar.activation(out=logd[:, j, cols], in_=capped[:, j, cols], func=ACT.Ln, bias=1.0)
             nc.vector.tensor_tensor(out=en2[:, :, cols], in0=pre[:, :, cols], in1=logd[:, :, cols], op=ALU.max)
             if h == 1:
                 quantize_half(halves[0])
+                second_layer_half(0)
             nc.vector.tensor_copy(out=en2_grouped[:, cols, :], in_=en2[:, :, cols].rearrange("p j n -> p n j"))
         quantize_half(halves[1])
-        nc.scalar.activation(out=warm_out[:], in_=warm_in[:], func=ACT.Exp)
         eps_t = const.tile([P, ROWS, P], F32)
         nc.scalar.copy(out=eps_t[:], in_=eps_bank[:])
+        nc.scalar.activation(out=warm_out[:], in_=warm_in[:], func=ACT.Exp)
+        second_layer_half(1)
 
-        heads = [None, None]
-        for w in (1, 0):
-            head = psum.tile([P, N], F32, tag="bank", name="head")
-            cols = slice(C * w, C * (w + 1))
-            nc.tensor.matmul_mx(
-                out=head[:],
-                lhsT=wmv_codes[:, cols].bitcast(FP8X4),
-                lhsT_scale=wmv_scales[:, cols],
-                rhs=en2_codes[:].bitcast(FP8X4),
-                rhs_scale=en2_scales[:],
-                start=True,
-                stop=True,
-            )
-            heads[w] = head
-
-        stats = tail.tile([P, 2, 6], F32)
         mean_var = tail.tile([P, 2, 2], F32)
+        for h in range(2):
+            stats_half(h)
         for w in (1, 0):
-            nc.vector.bn_stats(out=stats[:, w, :], in_=heads[w][:])
-        for w in (1, 0):
-            nc.vector.bn_aggr(out=mean_var[:, w, :], in_=stats[:, w, :])
+            nc.vector.bn_aggr(out=mean_var[:, w, :], in_=stats[:, w, :, :])
         var_eps = tail.tile([P, 2], F32)
         nc.vector.tensor_scalar(out=var_eps[:], in0=mean_var[:, :, 1], scalar1=BN_EPS, scalar2=None, op0=ALU.add)
         rstd = tail.tile([P, 2], F32)
@@ -256,13 +263,14 @@ def tile_model_pa_k_kernel(tc, en1, eps, W2, b2, Wm, Wv, gm, betam, gv, betav, o
         mean = tail.tile([P, N], F32)
         z_t = tail.tile([P, N], F32)
         eps_cols = eps_t[:].rearrange("c i p -> c (i p)")
-        for cols in halves:
+        for h, cols in enumerate(halves):
             nc.scalar.activation(
-                out=std[:, cols], in_=heads[1][:, cols], func=ACT.Exp, bias=shift[:, 1:2], scale=scale[:, 1:2]
+                out=std[:, cols], in_=heads[1][h][:], func=ACT.Exp, bias=shift[:, 1:2], scale=scale[:, 1:2]
             )
-        nc.vector.tensor_scalar(
-            out=mean[:], in0=heads[0][:], scalar1=scale[:, 0:1], scalar2=shift[:, 0:1], op0=ALU.mult, op1=ALU.add
-        )
+            nc.vector.tensor_scalar(
+                out=mean[:, cols], in0=heads[0][h][:], scalar1=scale[:, 0:1], scalar2=shift[:, 0:1],
+                op0=ALU.mult, op1=ALU.add,
+            )
         for cols in halves:
             nc.vector.tensor_tensor(out=noise[:, cols], in0=std[:, cols], in1=eps_cols[:, cols], op=ALU.mult)
         for cols in halves:

from contextlib import ExitStack

import concourse.mybir as mybir
from concourse.masks import make_identity

F32 = mybir.dt.float32
BF16 = mybir.dt.bfloat16
U32 = mybir.dt.uint32
U8 = mybir.dt.uint8
FP8X4 = mybir.dt.float8_e4m3fn_x4
ALU = mybir.AluOpType
ACT = mybir.ActivationFunctionType

P = 128
N = 512
E1 = 16384
E2 = 512
C = 128
K_PASS = 512
PASSES = E1 // K_PASS
ROWS = 4
WORDS = K_PASS // 2
LOADS = [1, 1] + [2] * ((PASSES - 2) // 2)
MAX_LOAD = 2 * K_PASS
RAW_BUFS = 4
BN_EPS = 1e-5
EXP_CAP = 1.0e13

FLOPS = 2 * N * E1 * E2 + 2 * 2 * N * E2 * C


def transpose_bank(nc, psum, words, first_word, b, ident):
    bank = psum.tile([P, 2, 2, P], F32, tag="bank", name="bank")
    for s in range(2):
        for u in range(2):
            start = first_word + P * u
            nc.tensor.transpose(bank[:, s, u, :], words[:, 2 * b + s, start : start + P], ident[:])
    return bank


def bank_to_grouped(copy, grouped, b, bank):
    half = grouped[:].bitcast(F32)[:, 4 * P * b : 4 * P * (b + 1)]
    copy(
        out=half.rearrange("q (s r u) -> q s r u", s=2, u=2),
        in_=bank[:].rearrange("q s u r -> q s r u"),
    )


def tile_model_pa_k_kernel(tc, en1, eps, W2, b2, Wm, Wv, gm, betam, gv, betav, out):
    nc = tc.nc
    with ExitStack() as ctx:
        ctx.enter_context(tc.manual_schedule())
        const = ctx.enter_context(tc.tile_pool(name="const", bufs=1))
        raw = ctx.enter_context(tc.tile_pool(name="raw", bufs=RAW_BUFS))
        stage = ctx.enter_context(tc.tile_pool(name="stage", bufs=3))
        tail = ctx.enter_context(tc.tile_pool(name="tail", bufs=1))
        psum_acc = ctx.enter_context(tc.psum_pool(name="psum_acc", bufs=1))
        psum = ctx.enter_context(tc.psum_pool(name="psum", bufs=4))

        en1_rows = en1.rearrange("(p i) k -> p i k", i=ROWS)
        w2_rows = W2.rearrange("(p i) k -> p i k", i=ROWS)

        ident = const.tile([P, P], F32)
        make_identity(nc, ident[:])
        ident_bf16 = const.tile([P, P], BF16)
        nc.vector.tensor_copy(out=ident_bf16[:], in_=ident[:])

        b2_raw = const.tile([P, ROWS], BF16)
        with nc.allow_non_contiguous_dma(reason="four elements a partition, once"):
            nc.gpsimd.dma_start(out=b2_raw[:], in_=b2.rearrange("(p i) -> p i", i=ROWS))
        b2_f32 = const.tile([P, ROWS], F32)
        nc.gpsimd.tensor_scalar(out=b2_f32[:], in0=b2_raw[:], scalar1=1.0, scalar2=0.0, op0=ALU.mult, op1=ALU.add)

        rows_raw = const.tile([P, ROWS * C], BF16)
        nc.vector.memset(rows_raw[:], 0.0)
        wmv_raw = const.tile([P, 2, E2], BF16)
        eps_raw = const.tile([P, ROWS, C], BF16)

        acc = [psum_acc.tile([P, N], F32, name="acc%d" % j) for j in range(ROWS)]

        def multiply(g, x_codes, x_scales, w_codes, w_scales):
            for j in range(ROWS):
                cols = slice(P * j, P * (j + 1))
                nc.tensor.matmul_mx(
                    out=acc[j][:],
                    lhsT=w_codes[:, cols].bitcast(FP8X4),
                    lhsT_scale=w_scales[:, cols],
                    rhs=x_codes[:].bitcast(FP8X4),
                    rhs_scale=x_scales[:],
                    start=(g == 0),
                    stop=(g == PASSES - 1),
                )

        first_passes = [sum(LOADS[:n]) for n in range(len(LOADS))]
        x_raws, w_raws = {}, {}

        def load_x(n):
            k_cols = slice(K_PASS * first_passes[n], K_PASS * (first_passes[n] + LOADS[n]))
            x_raws[n] = raw.tile([P, ROWS, MAX_LOAD], BF16, name="x_raw")
            nc.sync.dma_start(out=x_raws[n][:, :, : K_PASS * LOADS[n]], in_=en1_rows[:, :, k_cols])

        def load_w(n):
            k_cols = slice(K_PASS * first_passes[n], K_PASS * (first_passes[n] + LOADS[n]))
            w_raws[n] = raw.tile([P, ROWS, MAX_LOAD], BF16, name="w_raw")
            nc.scalar.dma_start(out=w_raws[n][:, :, : K_PASS * LOADS[n]], in_=w2_rows[:, :, k_cols])

        for n in range(RAW_BUFS):
            load_x(n)
            load_w(n)

        warm_in = const.tile([P, 1], F32)
        warm_out = const.tile([P, 1], F32)
        nc.vector.memset(warm_in[:], 0.0)
        nc.scalar.activation(out=warm_out[:], in_=warm_in[:], func=ACT.Exp)
        neg_half = const.tile([P, 2], F32)
        nc.vector.memset(neg_half[:], -0.5)

        g = 0
        for load, passes in enumerate(LOADS):
            x_raw, w_raw = x_raws.pop(load), w_raws.pop(load)
            for t in range(passes):
                x_banks = [transpose_bank(nc, psum, x_raw[:].bitcast(F32), WORDS * t, b, ident) for b in range(2)]
                w_banks = [transpose_bank(nc, psum, w_raw[:].bitcast(F32), WORDS * t, b, ident) for b in range(2)]
                if g > 0:
                    multiply(g - 1, x_codes, x_scales, w_codes, w_scales)

                x_grouped = stage.tile([P, 4 * N], BF16, align_bytes=64)
                w_grouped = stage.tile([P, 4 * E2], BF16, align_bytes=64)
                bank_to_grouped(nc.scalar.copy, x_grouped, 0, x_banks[0])
                bank_to_grouped(nc.vector.tensor_copy, x_grouped, 1, x_banks[1])
                bank_to_grouped(nc.scalar.copy, w_grouped, 0, w_banks[0])
                bank_to_grouped(nc.scalar.copy, w_grouped, 1, w_banks[1])

                x_codes = stage.tile([P, N], U32, align_bytes=64)
                x_scales = stage.tile([P, N], U8, align_bytes=64)
                w_codes = stage.tile([P, E2], U32, align_bytes=64)
                w_scales = stage.tile([P, E2], U8, align_bytes=64)
                nc.vector.quantize_mx(out=x_codes[:].bitcast(FP8X4), scales=x_scales[:], in_=x_grouped[:])
                nc.vector.quantize_mx(out=w_codes[:].bitcast(FP8X4), scales=w_scales[:], in_=w_grouped[:])
                g += 1

            if load + RAW_BUFS < len(LOADS):
                load_x(load + RAW_BUFS)
                load_w(load + RAW_BUFS)
            elif load + RAW_BUFS == len(LOADS):
                nc.sync.dma_start(out=wmv_raw[:, 0, :], in_=Wm)
                nc.sync.dma_start(out=wmv_raw[:, 1, :], in_=Wv)
                nc.sync.dma_start(out=eps_raw[:], in_=eps.rearrange("(p i) c -> p i c", i=ROWS))
                for i, vec in enumerate((gm, betam, gv, betav)):
                    nc.sync.dma_start(out=rows_raw[0:1, C * i : C * (i + 1)], in_=vec.rearrange("(o c) -> o c", o=1))
        multiply(PASSES - 1, x_codes, x_scales, w_codes, w_scales)

        expd = tail.tile([P, ROWS, N], F32)
        capped = tail.tile([P, ROWS, N], F32)
        pre = tail.tile([P, ROWS, N], BF16)
        logd = tail.tile([P, ROWS, N], BF16)
        for j in range(ROWS):
            bias = b2_f32[:, j : j + 1]
            nc.scalar.activation(out=expd[:, j, :], in_=acc[j][:], func=ACT.Exp, bias=bias)
            nc.vector.tensor_scalar(out=pre[:, j, :], in0=acc[j][:], scalar1=bias, scalar2=None, op0=ALU.add)
            nc.vector.tensor_scalar(out=capped[:, j, :], in0=expd[:, j, :], scalar1=EXP_CAP, scalar2=None, op0=ALU.min)

        wmv_words = wmv_raw[:].bitcast(F32).rearrange("c w (p u) -> c w u p", u=2)
        wmv_bank = psum.tile([P, 2, 2, P], F32, tag="bank", name="wmv_bank")
        for w in range(2):
            for u in range(2):
                nc.tensor.transpose(wmv_bank[:, w, u, :], wmv_words[:, w, u, :], ident[:])
        eps_bank = psum.tile([P, ROWS, P], BF16, tag="bank", name="eps_bank")
        for i in range(ROWS):
            nc.tensor.transpose(eps_bank[:, i, :], eps_raw[:, i, :], ident_bf16[:])
        rows_bank = psum.tile([P, 4, P], BF16, tag="bank", name="rows_bank")
        for i in range(4):
            nc.tensor.transpose(rows_bank[:, i, :], rows_raw[:, C * i : C * (i + 1)], ident_bf16[:])
        wmv_grouped = const.tile([P, 2 * C * 4], BF16, align_bytes=64)
        nc.vector.tensor_copy(
            out=wmv_grouped[:].bitcast(F32).rearrange("q (w c u) -> q w c u", w=2, u=2),
            in_=wmv_bank[:].rearrange("q w u c -> q w c u"),
        )
        wmv_codes = const.tile([P, 2 * C], U32, align_bytes=64)
        wmv_scales = const.tile([P, 2 * C], U8, align_bytes=64)
        params = const.tile([P, 2, 2], F32)
        for w, factor in enumerate((1.0, 0.5)):
            nc.vector.tensor_scalar(
                out=params[:, :, w], in0=rows_bank[:, 2 * w : 2 * w + 2, 0], scalar1=factor, scalar2=None, op0=ALU.mult
            )
        gamma = params[:, 0, :]
        beta = params[:, 1, :]
        nc.vector.quantize_mx(out=wmv_codes[:].bitcast(FP8X4), scales=wmv_scales[:], in_=wmv_grouped[:])

        halves = [slice(0, N // 2), slice(N // 2, N)]
        en2 = tail.tile([P, ROWS, N], BF16)
        en2_grouped = tail.tile([P, N, ROWS], BF16, align_bytes=64)
        en2_codes = tail.tile([P, N], U32, align_bytes=64)
        en2_scales = tail.tile([P, N], U8, align_bytes=64)

        def quantize_half(cols):
            nc.vector.quantize_mx(
                out=en2_codes[:, cols].bitcast(FP8X4), scales=en2_scales[:, cols],
                in_=en2_grouped[:, cols, :].rearrange("p n j -> p (n j)"),
            )

        heads = [{}, {}]
        stats = tail.tile([P, 2, 2, 6], F32)

        def second_layer_half(h):
            cols = halves[h]
            for w in (1, 0):
                heads[w][h] = psum.tile([P, N // 2], F32, tag="bank", name="head")
                w_cols = slice(C * w, C * (w + 1))
                nc.tensor.matmul_mx(
                    out=heads[w][h][:],
                    lhsT=wmv_codes[:, w_cols].bitcast(FP8X4),
                    lhsT_scale=wmv_scales[:, w_cols],
                    rhs=en2_codes[:, cols].bitcast(FP8X4),
                    rhs_scale=en2_scales[:, cols],
                    start=True,
                    stop=True,
                )

        def stats_half(h):
            for w in (1, 0):
                nc.vector.bn_stats(out=stats[:, w, h, :], in_=heads[w][h][:])

        for h, cols in enumerate(halves):
            for j in range(ROWS):
                nc.scalar.activation(out=logd[:, j, cols], in_=capped[:, j, cols], func=ACT.Ln, bias=1.0)
            nc.vector.tensor_tensor(out=en2[:, :, cols], in0=pre[:, :, cols], in1=logd[:, :, cols], op=ALU.max)
            if h == 1:
                quantize_half(halves[0])
                second_layer_half(0)
            nc.vector.tensor_copy(out=en2_grouped[:, cols, :], in_=en2[:, :, cols].rearrange("p j n -> p n j"))
        quantize_half(halves[1])
        eps_t = const.tile([P, ROWS, P], F32)
        nc.scalar.copy(out=eps_t[:], in_=eps_bank[:])
        nc.scalar.activation(out=warm_out[:], in_=warm_in[:], func=ACT.Exp)
        second_layer_half(1)

        mean_var = tail.tile([P, 2, 2], F32)
        for h in range(2):
            stats_half(h)
        for w in (1, 0):
            nc.vector.bn_aggr(out=mean_var[:, w, :], in_=stats[:, w, :, :])
        var_eps = tail.tile([P, 2], F32)
        nc.vector.tensor_scalar(out=var_eps[:], in0=mean_var[:, :, 1], scalar1=BN_EPS, scalar2=None, op0=ALU.add)
        rstd = tail.tile([P, 2], F32)
        nc.gpsimd.tensor_tensor(out=rstd[:], in0=var_eps[:], in1=neg_half[:], op=ALU.pow)
        neg_mean_gamma = tail.tile([P, 2], F32)
        nc.vector.scalar_tensor_tensor(
            out=neg_mean_gamma[:], in0=mean_var[:, :, 0], scalar=-1.0, in1=gamma, op0=ALU.mult, op1=ALU.mult
        )
        scale = tail.tile([P, 2], F32)
        nc.vector.tensor_tensor(out=scale[:], in0=rstd[:], in1=gamma, op=ALU.mult)
        shift = tail.tile([P, 2], F32)
        for w in (1, 0):
            one = slice(w, w + 1)
            nc.vector.scalar_tensor_tensor(
                out=shift[:, one], in0=rstd[:, one], scalar=neg_mean_gamma[:, one], in1=beta[:, one],
                op0=ALU.mult, op1=ALU.add,
            )

        std = tail.tile([P, N], F32)
        noise = tail.tile([P, N], F32)
        mean = tail.tile([P, N], F32)
        z_t = tail.tile([P, N], F32)
        eps_cols = eps_t[:].rearrange("c i p -> c (i p)")
        for h, cols in enumerate(halves):
            nc.scalar.activation(
                out=std[:, cols], in_=heads[1][h][:], func=ACT.Exp, bias=shift[:, 1:2], scale=scale[:, 1:2]
            )
            nc.vector.tensor_scalar(
                out=mean[:, cols], in0=heads[0][h][:], scalar1=scale[:, 0:1], scalar2=shift[:, 0:1],
                op0=ALU.mult, op1=ALU.add,
            )
        for cols in halves:
            nc.vector.tensor_tensor(out=noise[:, cols], in0=std[:, cols], in1=eps_cols[:, cols], op=ALU.mult)
        for cols in halves:
            nc.vector.tensor_tensor(out=z_t[:, cols], in0=mean[:, cols], in1=noise[:, cols], op=ALU.add)

        out_rows = out.rearrange("(p i) c -> p i c", i=ROWS)
        for h, (copy, dma) in enumerate(((nc.scalar.copy, nc.scalar.dma_start), (nc.vector.tensor_copy, nc.sync.dma_start))):
            z_bank = psum.tile([P, 2, C], F32, tag="bank", name="z_bank")
            for s in range(2):
                i = 2 * h + s
                nc.tensor.transpose(z_bank[:, s, :], z_t[:, P * i : P * (i + 1)], ident[:])
            z = tail.tile([P, 2, C], F32, name="z%d" % h)
            copy(out=z[:], in_=z_bank[:])
            dma(out=out_rows[:, 2 * h : 2 * h + 2, :], in_=z[:])
